import numpy as np
import ml_dtypes

BF16 = ml_dtypes.bfloat16


def bf(x):
    return np.asarray(x, np.float32).astype(BF16)


def f32(x):
    return np.asarray(x, np.float32)


def f64(x):
    return np.asarray(x).astype(np.float64)


def striped(idx):
    return np.tile(idx.reshape(-1, 16).T, (8, 1))


D, Q, C, S, B, T, N = 128, 4, 512, 2048, 2, 256, 1024
BASE, EPS = 10000.0, 1e-6


def freq_scale():
    s = f32(1.0) / f32(BASE) ** (f32(np.arange(D)) / f32(D))
    return f32(np.concatenate([np.ones(D)] + [s] * (Q - 1)).reshape(C, 1))


def rope_table():
    inv = f32(1.0) / f32(BASE) ** (f32(np.arange(0, D, 2)) / f32(D))
    fr = f32(np.arange(T))[:, None] * inv[None, :]
    a = np.concatenate([np.sin(f64(fr)), np.cos(f64(fr))], axis=1)
    return f32(np.tile(a.T, (1, N // T)))


def setup_inputs():
    return {"x": f32(0.1 * np.random.standard_normal((C, S))), "sc": freq_scale(), "ang": rope_table(), "offs": striped(np.random.permutation(np.tile(np.arange(S), 2))[:N])}


def reference(x, sc, ang, offs):
    idx = offs[:16].T.reshape(-1)
    v = (f64(x)[:, idx] * f64(sc)).reshape(Q, D, N)
    n = np.sqrt((v * v).sum(axis=0) + EPS)
    return (v / n * f64(ang)).reshape(C, N)

@@ -1,0 +1,62 @@
+import concourse.mybir as mybir
+
+P = 128
+Q = 4
+VOCAB = 2048
+N = 1024
+EPS = 1e-6
+
+F32 = mybir.dt.float32
+U16 = mybir.dt.uint16
+MULT = mybir.AluOpType.mult
+ADD = mybir.AluOpType.add
+FUNC = mybir.ActivationFunctionType
+
+
+def tile_quaterniontransformer_kernel(tc, x, sc, ang, offs, out):
+    nc = tc.nc
+    with tc.tile_pool(name="held", bufs=1) as held:
+        offsets = held.tile([P, N // 16], U16, name="offsets")
+        nc.sync.dma_start(offsets[:], offs)
+
+        scale = held.tile([P, Q], F32, name="scale")
+        with nc.allow_non_contiguous_dma(reason="512 scales, one to a partition and component"):
+            nc.scalar.dma_start(scale[:], sc.rearrange("(q d) o -> d (q o)", q=Q))
+
+        tables = []
+        for q in range(Q):
+            table = held.tile([P, VOCAB], F32, name=f"table{q}")
+            nc.sync.dma_start(table[:], x[q * P : (q + 1) * P, :])
+            tables.append(table)
+
+        angle = held.tile([P, N], F32, name="angle")
+        nc.sync.dma_start(angle[:], ang)
+
+        scale_rows = held.tile([P, Q, N], F32, name="scale_rows")
+        for q in range(Q):
+            nc.scalar.copy(scale_rows[:, q, :], scale[:, q : q + 1].to_broadcast([P, N]))
+
+        v = held.tile([P, Q, N], F32, name="v")
+        squares = held.tile([P, Q, N], F32, name="squares")
+        for q in range(Q):
+            nc.vector.tensor_tensor(
+                v[:, q, :],
+                tables[q][:].indirect(offsets[:]),
+                scale_rows[:, q, :],
+                MULT,
+            )
+            nc.scalar.activation(squares[:, q, :], v[:, q, :], FUNC.Square)
+
+        norm2 = held.tile([P, N], F32, name="norm2")
+        nc.vector.tensor_tensor(norm2[:], squares[:, 0, :], squares[:, 1, :], ADD)
+        nc.vector.tensor_tensor(norm2[:], norm2[:], squares[:, 2, :], ADD)
+        nc.vector.tensor_tensor(norm2[:], norm2[:], squares[:, 3, :], ADD)
+
+        factor = held.tile([P, N], F32, name="factor")
+        nc.scalar.activation(factor[:], norm2[:], FUNC.Abs_reciprocal_sqrt, bias=EPS)
+        nc.vector.tensor_tensor(factor[:], factor[:], angle[:], MULT)
+
+        result = held.tile([P, Q, N], F32, name="result")
+        for q in range(Q):
+            nc.vector.tensor_tensor(result[:, q, :], v[:, q, :], factor[:], MULT)
+            nc.sync.dma_start(out[q * P : (q + 1) * P, :], result[:, q, :])

@@ -1,21 +1,29 @@
 import concourse.mybir as mybir
+from concourse.masks import make_identity
 
 P = 128
 Q = 4
 VOCAB = 2048
 N = 1024
 EPS = 1e-6
+PIECE = 256
+HALF = 512
+PIECES = N // PIECE
+WARMING = 10
 
 F32 = mybir.dt.float32
 U16 = mybir.dt.uint16
 MULT = mybir.AluOpType.mult
-ADD = mybir.AluOpType.add
 FUNC = mybir.ActivationFunctionType
 
 
 def tile_quaterniontransformer_kernel(tc, x, sc, ang, offs, out):
     nc = tc.nc
-    with tc.tile_pool(name="held", bufs=1) as held:
+    with (
+        tc.tile_pool(name="held", bufs=1) as held,
+        tc.tile_pool(name="ring", bufs=PIECES) as ring,
+        tc.psum_pool(name="psum", bufs=1) as psum,
+    ):
         offsets = held.tile([P, N // 16], U16, name="offsets")
         nc.sync.dma_start(offsets[:], offs)
 
@@ -32,31 +40,53 @@ def tile_quaterniontransformer_kernel(tc, x, sc, ang, offs, out):
         angle = held.tile([P, N], F32, name="angle")
         nc.sync.dma_start(angle[:], ang)
 
-        scale_rows = held.tile([P, Q, N], F32, name="scale_rows")
+        ones = held.tile([P, 1], F32, name="ones")
+        nc.gpsimd.memset(ones[:], 1.0)
+        nc.scalar.activation(ones[:], ones[:], FUNC.Abs_reciprocal_sqrt)
+
+        identity = held.tile([P, P], F32, name="identity")
+        make_identity(nc, identity[:])
+
+        unread = psum.tile([P, P], F32, name="unread")
+        for i in range(WARMING):
+            nc.tensor.matmul(unread[:], identity[:], identity[:], start=True, stop=True)
+
+        scale_rows = held.tile([P, Q, HALF], F32, name="scale_rows")
         for q in range(Q):
-            nc.scalar.copy(scale_rows[:, q, :], scale[:, q : q + 1].to_broadcast([P, N]))
+            nc.scalar.copy(scale_rows[:, q, :], scale[:, q : q + 1].to_broadcast([P, HALF]))
 
         v = held.tile([P, Q, N], F32, name="v")
         squares = held.tile([P, Q, N], F32, name="squares")
+        norm2 = [psum.tile([P, PIECE], F32, name=f"norm2_{p}") for p in range(PIECES)]
+
         for q in range(Q):
+            width = PIECE if q == Q - 1 else HALF
+            for first in range(0, N, width):
+                cols = slice(first, first + width)
+                nc.vector.tensor_tensor(
+                    v[:, q, cols],
+                    tables[q][:].indirect(offsets[:, first // 16 : (first + width) // 16]),
+                    scale_rows[:, q, :width],
+                    MULT,
+                )
+                nc.scalar.activation(squares[:, q, cols], v[:, q, cols], FUNC.Square)
+                for p in range(first // PIECE, (first + width) // PIECE):
+                    nc.tensor.matmul(
+                        norm2[p][:],
+                        identity[:],
+                        squares[:, q, p * PIECE : (p + 1) * PIECE],
+                        start=(q == 0),
+                        stop=(q == Q - 1),
+                    )
+
+        out_dqj = out.rearrange("(q d) j -> d q j", q=Q)
+        for p in range(PIECES):
+            cols = slice(p * PIECE, (p + 1) * PIECE)
+            factor = ring.tile([P, PIECE], F32, name="factor")
+            nc.scalar.activation(factor[:], norm2[p][:], FUNC.Abs_reciprocal_sqrt, bias=EPS)
+            nc.vector.tensor_tensor(factor[:], factor[:], angle[:, cols], MULT)
+            result = ring.tile([P, Q, PIECE], F32, name="result")
             nc.vector.tensor_tensor(
-                v[:, q, :],
-                tables[q][:].indirect(offsets[:]),
-                scale_rows[:, q, :],
-                MULT,
+                result[:], v[:, :, cols], factor[:].unsqueeze(1).to_broadcast([P, Q, PIECE]), MULT
             )
-            nc.scalar.activation(squares[:, q, :], v[:, q, :], FUNC.Square)
-
-        norm2 = held.tile([P, N], F32, name="norm2")
-        nc.vector.tensor_tensor(norm2[:], squares[:, 0, :], squares[:, 1, :], ADD)
-        nc.vector.tensor_tensor(norm2[:], norm2[:], squares[:, 2, :], ADD)
-        nc.vector.tensor_tensor(norm2[:], norm2[:], squares[:, 3, :], ADD)
-
-        factor = held.tile([P, N], F32, name="factor")
-        nc.scalar.activation(factor[:], norm2[:], FUNC.Abs_reciprocal_sqrt, bias=EPS)
-        nc.vector.tensor_tensor(factor[:], factor[:], angle[:], MULT)
-
-        result = held.tile([P, Q, N], F32, name="result")
-        for q in range(Q):
-            nc.vector.tensor_tensor(result[:, q, :], v[:, q, :], factor[:], MULT)
-            nc.sync.dma_start(out[q * P : (q + 1) * P, :], result[:, q, :])
+            nc.sync.dma_start(out_dqj[:, :, cols], result[:])

@@ -87,6 +87,10 @@ def tile_quaterniontransformer_kernel(tc, x, sc, ang, offs, out):
             nc.vector.tensor_tensor(factor[:], factor[:], angle[:, cols], MULT)
             result = ring.tile([P, Q, PIECE], F32, name="result")
             nc.vector.tensor_tensor(
-                result[:], v[:, :, cols], factor[:].unsqueeze(1).to_broadcast([P, Q, PIECE]), MULT
+                result[:, : Q - 1, :],
+                v[:, : Q - 1, cols],
+                factor[:].unsqueeze(1).to_broadcast([P, Q - 1, PIECE]),
+                MULT,
             )
+            nc.gpsimd.tensor_tensor(result[:, Q - 1, :], v[:, Q - 1, cols], factor[:], MULT)
             nc.sync.dma_start(out_dqj[:, :, cols], result[:])

@@ -6,7 +6,7 @@ Q = 4
 VOCAB = 2048
 N = 1024
 EPS = 1e-6
-PIECE = 256
+PIECE = 128
 HALF = 512
 PIECES = N // PIECE
 WARMING = 10
@@ -47,9 +47,10 @@ def tile_quaterniontransformer_kernel(tc, x, sc, ang, offs, out):
         identity = held.tile([P, P], F32, name="identity")
         make_identity(nc, identity[:])
 
-        unread = psum.tile([P, P], F32, name="unread")
+        norm2 = [psum.tile([P, PIECE], F32, name=f"norm2_{p}") for p in range(PIECES)]
+
         for i in range(WARMING):
-            nc.tensor.matmul(unread[:], identity[:], identity[:], start=True, stop=True)
+            nc.tensor.matmul(norm2[0][:], identity[:], identity[:], start=True, stop=True)
 
         scale_rows = held.tile([P, Q, HALF], F32, name="scale_rows")
         for q in range(Q):
@@ -57,7 +58,6 @@ def tile_quaterniontransformer_kernel(tc, x, sc, ang, offs, out):
 
         v = held.tile([P, Q, N], F32, name="v")
         squares = held.tile([P, Q, N], F32, name="squares")
-        norm2 = [psum.tile([P, PIECE], F32, name=f"norm2_{p}") for p in range(PIECES)]
 
         for q in range(Q):
             width = PIECE if q == Q - 1 else HALF
@@ -87,10 +87,6 @@ def tile_quaterniontransformer_kernel(tc, x, sc, ang, offs, out):
             nc.vector.tensor_tensor(factor[:], factor[:], angle[:, cols], MULT)
             result = ring.tile([P, Q, PIECE], F32, name="result")
             nc.vector.tensor_tensor(
-                result[:, : Q - 1, :],
-                v[:, : Q - 1, cols],
-                factor[:].unsqueeze(1).to_broadcast([P, Q - 1, PIECE]),
-                MULT,
+                result[:], v[:, :, cols], factor[:].unsqueeze(1).to_broadcast([P, Q, PIECE]), MULT
             )
-            nc.gpsimd.tensor_tensor(result[:, Q - 1, :], v[:, Q - 1, cols], factor[:], MULT)
             nc.sync.dma_start(out_dqj[:, :, cols], result[:])

@@ -6,10 +6,10 @@ Q = 4
 VOCAB = 2048
 N = 1024
 EPS = 1e-6
-PIECE = 128
+PIECE = 256
 HALF = 512
 PIECES = N // PIECE
-WARMING = 10
+WARMING = 16
 
 F32 = mybir.dt.float32
 U16 = mybir.dt.uint16
@@ -47,10 +47,9 @@ def tile_quaterniontransformer_kernel(tc, x, sc, ang, offs, out):
         identity = held.tile([P, P], F32, name="identity")
         make_identity(nc, identity[:])
 
-        norm2 = [psum.tile([P, PIECE], F32, name=f"norm2_{p}") for p in range(PIECES)]
-
+        unread = psum.tile([P, P], F32, name="unread")
         for i in range(WARMING):
-            nc.tensor.matmul(norm2[0][:], identity[:], identity[:], start=True, stop=True)
+            nc.tensor.matmul(unread[:], identity[:], identity[:], start=True, stop=True)
 
         scale_rows = held.tile([P, Q, HALF], F32, name="scale_rows")
         for q in range(Q):
@@ -58,6 +57,7 @@ def tile_quaterniontransformer_kernel(tc, x, sc, ang, offs, out):
 
         v = held.tile([P, Q, N], F32, name="v")
         squares = held.tile([P, Q, N], F32, name="squares")
+        norm2 = [psum.tile([P, PIECE], F32, name=f"norm2_{p}") for p in range(PIECES)]
 
         for q in range(Q):
             width = PIECE if q == Q - 1 else HALF

@@ -27,9 +27,8 @@ def tile_quaterniontransformer_kernel(tc, x, sc, ang, offs, out):
         offsets = held.tile([P, N // 16], U16, name="offsets")
         nc.sync.dma_start(offsets[:], offs)
 
-        scale = held.tile([P, Q], F32, name="scale")
-        with nc.allow_non_contiguous_dma(reason="512 scales, one to a partition and component"):
-            nc.scalar.dma_start(scale[:], sc.rearrange("(q d) o -> d (q o)", q=Q))
+        scale_in_rows = held.tile([Q, P], F32, name="scale_in_rows")
+        nc.scalar.dma_start(scale_in_rows[:], sc.rearrange("(q d) o -> q (d o)", q=Q))
 
         tables = []
         for q in range(Q):
@@ -46,6 +45,9 @@ def tile_quaterniontransformer_kernel(tc, x, sc, ang, offs, out):
 
         identity = held.tile([P, P], F32, name="identity")
         make_identity(nc, identity[:])
+
+        scale = psum.tile([P, Q], F32, name="scale")
+        nc.tensor.matmul(scale[:], scale_in_rows[:], identity[:Q, :Q], start=True, stop=True)
 
         unread = psum.tile([P, P], F32, name="unread")
         for i in range(WARMING):

@@ -9,7 +9,7 @@ EPS = 1e-6
 PIECE = 256
 HALF = 512
 PIECES = N // PIECE
-WARMING = 16
+WARMING = 8
 
 F32 = mybir.dt.float32
 U16 = mybir.dt.uint16

@@ -6,8 +6,8 @@ Q = 4
 VOCAB = 2048
 N = 1024
 EPS = 1e-6
-PIECE = 256
 HALF = 512
+PIECE = 256
 PIECES = N // PIECE
 WARMING = 8
 
@@ -27,8 +27,8 @@ def tile_quaterniontransformer_kernel(tc, x, sc, ang, offs, out):
         offsets = held.tile([P, N // 16], U16, name="offsets")
         nc.sync.dma_start(offsets[:], offs)
 
-        scale_in_rows = held.tile([Q, P], F32, name="scale_in_rows")
-        nc.scalar.dma_start(scale_in_rows[:], sc.rearrange("(q d) o -> q (d o)", q=Q))
+        sc_rows = held.tile([Q, P], F32, name="sc_rows")
+        nc.scalar.dma_start(sc_rows[:], sc.rearrange("(q d) o -> q (d o)", q=Q))
 
         tables = []
         for q in range(Q):
@@ -46,16 +46,16 @@ def tile_quaterniontransformer_kernel(tc, x, sc, ang, offs, out):
         identity = held.tile([P, P], F32, name="identity")
         make_identity(nc, identity[:])
 
-        scale = psum.tile([P, Q], F32, name="scale")
-        nc.tensor.matmul(scale[:], scale_in_rows[:], identity[:Q, :Q], start=True, stop=True)
+        sc_columns = psum.tile([P, Q], F32, name="sc_columns")
+        nc.tensor.matmul(sc_columns[:], sc_rows[:], identity[:Q, :Q], start=True, stop=True)
 
         unread = psum.tile([P, P], F32, name="unread")
         for i in range(WARMING):
             nc.tensor.matmul(unread[:], identity[:], identity[:], start=True, stop=True)
 
-        scale_rows = held.tile([P, Q, HALF], F32, name="scale_rows")
+        sc_spread = held.tile([P, Q, HALF], F32, name="sc_spread")
         for q in range(Q):
-            nc.scalar.copy(scale_rows[:, q, :], scale[:, q : q + 1].to_broadcast([P, HALF]))
+            nc.scalar.copy(sc_spread[:, q, :], sc_columns[:, q : q + 1].to_broadcast([P, HALF]))
 
         v = held.tile([P, Q, N], F32, name="v")
         squares = held.tile([P, Q, N], F32, name="squares")
@@ -68,7 +68,7 @@ def tile_quaterniontransformer_kernel(tc, x, sc, ang, offs, out):
                 nc.vector.tensor_tensor(
                     v[:, q, cols],
                     tables[q][:].indirect(offsets[:, first // 16 : (first + width) // 16]),
-                    scale_rows[:, q, :width],
+                    sc_spread[:, q, :width],
                     MULT,
                 )
                 nc.scalar.activation(squares[:, q, cols], v[:, q, cols], FUNC.Square)

@@ -22,6 +22,7 @@ def tile_quaterniontransformer_kernel(tc, x, sc, ang, offs, out):
     with (
         tc.tile_pool(name="held", bufs=1) as held,
         tc.tile_pool(name="ring", bufs=PIECES) as ring,
+        tc.tile_pool(name="pair", bufs=2) as pair,
         tc.psum_pool(name="psum", bufs=1) as psum,
     ):
         offsets = held.tile([P, N // 16], U16, name="offsets")
@@ -58,35 +59,57 @@ def tile_quaterniontransformer_kernel(tc, x, sc, ang, offs, out):
             nc.scalar.copy(sc_spread[:, q, :], sc_columns[:, q : q + 1].to_broadcast([P, HALF]))
 
         v = held.tile([P, Q, N], F32, name="v")
-        squares = held.tile([P, Q, N], F32, name="squares")
+        squares = held.tile([P, Q - 1, N], F32, name="squares")
         norm2 = [psum.tile([P, PIECE], F32, name=f"norm2_{p}") for p in range(PIECES)]
+        inverse = held.tile([P, N], F32, name="inverse")
 
-        for q in range(Q):
-            width = PIECE if q == Q - 1 else HALF
-            for first in range(0, N, width):
-                cols = slice(first, first + width)
-                nc.vector.tensor_tensor(
-                    v[:, q, cols],
-                    tables[q][:].indirect(offsets[:, first // 16 : (first + width) // 16]),
-                    sc_spread[:, q, :width],
-                    MULT,
-                )
-                nc.scalar.activation(squares[:, q, cols], v[:, q, cols], FUNC.Square)
-                for p in range(first // PIECE, (first + width) // PIECE):
-                    nc.tensor.matmul(
-                        norm2[p][:],
-                        identity[:],
-                        squares[:, q, p * PIECE : (p + 1) * PIECE],
-                        start=(q == 0),
-                        stop=(q == Q - 1),
-                    )
+        def look_up(q, first, width, squared):
+            cols = slice(first, first + width)
+            nc.vector.tensor_tensor(
+                v[:, q, cols],
+                tables[q][:].indirect(offsets[:, first // 16 : (first + width) // 16]),
+                sc_spread[:, q, :width],
+                MULT,
+            )
+            nc.scalar.activation(squared, v[:, q, cols], FUNC.Square)
+
+        def add_squares(q, p, squared):
+            nc.tensor.matmul(norm2[p][:], identity[:], squared, start=(q == 0), stop=(q == Q - 1))
+
+        def add_half(q, first):
+            for p in range(first // PIECE, (first + HALF) // PIECE):
+                add_squares(q, p, squares[:, q, p * PIECE : (p + 1) * PIECE])
+
+        def last_component(p):
+            squared = pair.tile([P, PIECE], F32, name="squared")
+            look_up(Q - 1, p * PIECE, PIECE, squared[:])
+            add_squares(Q - 1, p, squared[:])
+
+        def take_inverse(p):
+            nc.scalar.activation(
+                inverse[:, p * PIECE : (p + 1) * PIECE], norm2[p][:], FUNC.Abs_reciprocal_sqrt, bias=EPS
+            )
+
+        for q in range(Q - 1):
+            for first in range(0, N, HALF):
+                look_up(q, first, HALF, squares[:, q, first : first + HALF])
+                if (q, first) != (Q - 2, HALF):
+                    add_half(q, first)
+        last_component(0)
+        last_component(1)
+        take_inverse(0)
+        add_half(Q - 2, HALF)
+        last_component(2)
+        take_inverse(1)
+        last_component(3)
+        take_inverse(2)
+        take_inverse(3)
 
         out_dqj = out.rearrange("(q d) j -> d q j", q=Q)
         for p in range(PIECES):
             cols = slice(p * PIECE, (p + 1) * PIECE)
             factor = ring.tile([P, PIECE], F32, name="factor")
-            nc.scalar.activation(factor[:], norm2[p][:], FUNC.Abs_reciprocal_sqrt, bias=EPS)
-            nc.vector.tensor_tensor(factor[:], factor[:], angle[:, cols], MULT)
+            nc.vector.tensor_tensor(factor[:], inverse[:, cols], angle[:, cols], MULT)
             result = ring.tile([P, Q, PIECE], F32, name="result")
             nc.vector.tensor_tensor(
                 result[:], v[:, :, cols], factor[:].unsqueeze(1).to_broadcast([P, Q, PIECE]), MULT

@@ -111,7 +111,12 @@ def tile_quaterniontransformer_kernel(tc, x, sc, ang, offs, out):
             factor = ring.tile([P, PIECE], F32, name="factor")
             nc.vector.tensor_tensor(factor[:], inverse[:, cols], angle[:, cols], MULT)
             result = ring.tile([P, Q, PIECE], F32, name="result")
-            nc.vector.tensor_tensor(
-                result[:], v[:, :, cols], factor[:].unsqueeze(1).to_broadcast([P, Q, PIECE]), MULT
-            )
-            nc.sync.dma_start(out_dqj[:, :, cols], result[:])
+            if p < PIECES - 1:
+                nc.vector.tensor_tensor(
+                    result[:], v[:, :, cols], factor[:].unsqueeze(1).to_broadcast([P, Q, PIECE]), MULT
+                )
+                nc.sync.dma_start(out_dqj[:, :, cols], result[:])
+            else:
+                for q in range(Q):
+                    nc.vector.tensor_tensor(result[:, q, :], v[:, q, cols], factor[:], MULT)
+                    nc.sync.dma_start(out_dqj[:, q, cols], result[:, q, :])

@@ -22,6 +22,7 @@ def tile_quaterniontransformer_kernel(tc, x, sc, ang, offs, out):
     with (
         tc.tile_pool(name="held", bufs=1) as held,
         tc.tile_pool(name="ring", bufs=PIECES) as ring,
+        tc.tile_pool(name="first", bufs=1) as first_pool,
         tc.tile_pool(name="pair", bufs=2) as pair,
         tc.psum_pool(name="psum", bufs=1) as psum,
     ):
@@ -63,46 +64,48 @@ def tile_quaterniontransformer_kernel(tc, x, sc, ang, offs, out):
         norm2 = [psum.tile([P, PIECE], F32, name=f"norm2_{p}") for p in range(PIECES)]
         inverse = held.tile([P, N], F32, name="inverse")
 
-        def look_up(q, first, width, squared):
-            cols = slice(first, first + width)
+        def look_up(q, first, width, looked_up, squared):
             nc.vector.tensor_tensor(
-                v[:, q, cols],
+                looked_up,
                 tables[q][:].indirect(offsets[:, first // 16 : (first + width) // 16]),
                 sc_spread[:, q, :width],
                 MULT,
             )
-            nc.scalar.activation(squared, v[:, q, cols], FUNC.Square)
+            nc.scalar.activation(squared, looked_up, FUNC.Square)
 
-        def add_squares(q, p, squared):
-            nc.tensor.matmul(norm2[p][:], identity[:], squared, start=(q == 0), stop=(q == Q - 1))
-
-        def add_half(q, first):
-            for p in range(first // PIECE, (first + HALF) // PIECE):
-                add_squares(q, p, squares[:, q, p * PIECE : (p + 1) * PIECE])
-
-        def last_component(p):
-            squared = pair.tile([P, PIECE], F32, name="squared")
-            look_up(Q - 1, p * PIECE, PIECE, squared[:])
-            add_squares(Q - 1, p, squared[:])
+        def add_squares(p, squared, start=False, stop=False):
+            nc.tensor.matmul(norm2[p][:], identity[:], squared, start=start, stop=stop)
 
         def take_inverse(p):
             nc.scalar.activation(
                 inverse[:, p * PIECE : (p + 1) * PIECE], norm2[p][:], FUNC.Abs_reciprocal_sqrt, bias=EPS
             )
 
-        for q in range(Q - 1):
-            for first in range(0, N, HALF):
-                look_up(q, first, HALF, squares[:, q, first : first + HALF])
-                if (q, first) != (Q - 2, HALF):
-                    add_half(q, first)
-        last_component(0)
-        last_component(1)
+        def last_component(p, pool):
+            squared = pool.tile([P, PIECE], F32, name="squared", tag="squared")
+            look_up(Q - 1, p * PIECE, PIECE, v[:, Q - 1, p * PIECE : (p + 1) * PIECE], squared[:])
+            add_squares(p, squared[:], stop=(p < PIECES - 1))
+
+        for q, first in ((0, 0), (0, HALF), (1, 0), (1, HALF), (2, 0)):
+            cols = slice(first, first + HALF)
+            look_up(q, first, HALF, v[:, q, cols], squares[:, q, cols])
+            for p in range(first // PIECE, (first + HALF) // PIECE):
+                add_squares(p, squares[:, q, p * PIECE : (p + 1) * PIECE], start=(q == 0))
+
+        late = slice(N - PIECE, N)
+        cols = slice(HALF, HALF + PIECE)
+        look_up(2, HALF, PIECE, v[:, 2, cols], squares[:, 2, cols])
+        last_component(0, first_pool)
+        last_component(1, pair)
         take_inverse(0)
-        add_half(Q - 2, HALF)
-        last_component(2)
+        add_squares(2, squares[:, 2, cols])
+        last_component(2, pair)
         take_inverse(1)
-        last_component(3)
+        last_component(3, pair)
         take_inverse(2)
+        v_late = first_pool.tile([P, PIECE], F32, name="v_late", tag="squared")
+        look_up(2, N - PIECE, PIECE, v_late[:], squares[:, 2, late])
+        add_squares(PIECES - 1, squares[:, 2, late], stop=True)
         take_inverse(3)
 
         out_dqj = out.rearrange("(q d) j -> d q j", q=Q)
@@ -118,5 +121,6 @@ def tile_quaterniontransformer_kernel(tc, x, sc, ang, offs, out):
                 nc.sync.dma_start(out_dqj[:, :, cols], result[:])
             else:
                 for q in range(Q):
-                    nc.vector.tensor_tensor(result[:, q, :], v[:, q, cols], factor[:], MULT)
+                    looked_up = v_late[:] if q == 2 else v[:, q, cols]
+                    nc.vector.tensor_tensor(result[:, q, :], looked_up, factor[:], MULT)
                     nc.sync.dma_start(out_dqj[:, q, cols], result[:, q, :])

@@ -110,17 +110,21 @@ def tile_quaterniontransformer_kernel(tc, x, sc, ang, offs, out):
 
         out_dqj = out.rearrange("(q d) j -> d q j", q=Q)
         for p in range(PIECES):
-            cols = slice(p * PIECE, (p + 1) * PIECE)
+            first = p * PIECE
+            cols = slice(first, first + PIECE)
+            parts = [slice(0, PIECE // 4), slice(PIECE // 4, PIECE)]
             factor = ring.tile([P, PIECE], F32, name="factor")
-            nc.vector.tensor_tensor(factor[:], inverse[:, cols], angle[:, cols], MULT)
+            for part in parts:
+                there = slice(first + part.start, first + part.stop)
+                nc.vector.tensor_tensor(factor[:, part], inverse[:, there], angle[:, there], MULT)
+            together = 1 if p == PIECES - 1 else 2 if p == PIECES - 2 else Q
             result = ring.tile([P, Q, PIECE], F32, name="result")
-            if p < PIECES - 1:
-                nc.vector.tensor_tensor(
-                    result[:], v[:, :, cols], factor[:].unsqueeze(1).to_broadcast([P, Q, PIECE]), MULT
-                )
-                nc.sync.dma_start(out_dqj[:, :, cols], result[:])
-            else:
-                for q in range(Q):
-                    looked_up = v_late[:] if q == 2 else v[:, q, cols]
-                    nc.vector.tensor_tensor(result[:, q, :], looked_up, factor[:], MULT)
-                    nc.sync.dma_start(out_dqj[:, q, cols], result[:, q, :])
+            for q in range(0, Q, together):
+                group = slice(q, q + together)
+                for part in parts if q == 0 else [slice(0, PIECE)]:
+                    there = slice(first + part.start, first + part.stop)
+                    held_back = q == 2 and p == PIECES - 1
+                    looked_up = v_late[:, part].unsqueeze(1) if held_back else v[:, group, there]
+                    spread = factor[:, part].unsqueeze(1).to_broadcast([P, together, part.stop - part.start])
+                    nc.vector.tensor_tensor(result[:, group, part], looked_up, spread, MULT)
+                nc.sync.dma_start(out_dqj[:, group, cols], result[:, group, :])

@@ -22,8 +22,8 @@ def tile_quaterniontransformer_kernel(tc, x, sc, ang, offs, out):
     with (
         tc.tile_pool(name="held", bufs=1) as held,
         tc.tile_pool(name="ring", bufs=PIECES) as ring,
-        tc.tile_pool(name="first", bufs=1) as first_pool,
-        tc.tile_pool(name="pair", bufs=2) as pair,
+        tc.tile_pool(name="slot", bufs=1) as slot,
+        tc.tile_pool(name="turn", bufs=3) as turn,
         tc.psum_pool(name="psum", bufs=1) as psum,
     ):
         offsets = held.tile([P, N // 16], U16, name="offsets")
@@ -81,31 +81,37 @@ def tile_quaterniontransformer_kernel(tc, x, sc, ang, offs, out):
                 inverse[:, p * PIECE : (p + 1) * PIECE], norm2[p][:], FUNC.Abs_reciprocal_sqrt, bias=EPS
             )
 
-        def last_component(p, pool):
-            squared = pool.tile([P, PIECE], F32, name="squared", tag="squared")
-            look_up(Q - 1, p * PIECE, PIECE, v[:, Q - 1, p * PIECE : (p + 1) * PIECE], squared[:])
-            add_squares(p, squared[:], stop=(p < PIECES - 1))
+        def piece(p):
+            return slice(p * PIECE, (p + 1) * PIECE)
 
-        for q, first in ((0, 0), (0, HALF), (1, 0), (1, HALF), (2, 0)):
-            cols = slice(first, first + HALF)
-            look_up(q, first, HALF, v[:, q, cols], squares[:, q, cols])
-            for p in range(first // PIECE, (first + HALF) // PIECE):
-                add_squares(p, squares[:, q, p * PIECE : (p + 1) * PIECE], start=(q == 0))
+        def look_up_in_turn(q, p, looked_up, stop):
+            squared = turn.tile([P, PIECE], F32, name="squared")
+            look_up(q, p * PIECE, PIECE, looked_up, squared[:])
+            add_squares(p, squared[:], stop=stop)
 
-        late = slice(N - PIECE, N)
-        cols = slice(HALF, HALF + PIECE)
-        look_up(2, HALF, PIECE, v[:, 2, cols], squares[:, 2, cols])
-        last_component(0, first_pool)
-        last_component(1, pair)
+        for q in (0, 1):
+            for first in (0, HALF):
+                half = slice(first, first + HALF)
+                look_up(q, first, HALF, v[:, q, half], squares[:, q, half])
+                for p in range(first // PIECE, (first + HALF) // PIECE):
+                    add_squares(p, squares[:, q, piece(p)], start=(q == 0))
+        look_up(2, 0, PIECE, v[:, 2, piece(0)], squares[:, 2, piece(0)])
+        add_squares(0, squares[:, 2, piece(0)])
+        squared1 = slot.tile([P, PIECE], F32, name="squared1", tag="slot")
+        look_up(2, PIECE, PIECE, v[:, 2, piece(1)], squared1[:])
+        add_squares(1, squared1[:])
+        look_up(2, 2 * PIECE, PIECE, v[:, 2, piece(2)], squares[:, 2, piece(2)])
+
+        look_up_in_turn(3, 0, v[:, 3, piece(0)], True)
+        look_up_in_turn(3, 1, v[:, 3, piece(1)], True)
+        add_squares(2, squares[:, 2, piece(2)])
+        look_up_in_turn(3, 2, v[:, 3, piece(2)], True)
         take_inverse(0)
-        add_squares(2, squares[:, 2, cols])
-        last_component(2, pair)
+        look_up_in_turn(3, 3, v[:, 3, piece(3)], False)
         take_inverse(1)
-        last_component(3, pair)
+        v_late = slot.tile([P, PIECE], F32, name="v_late", tag="slot")
+        look_up_in_turn(2, 3, v_late[:], True)
         take_inverse(2)
-        v_late = first_pool.tile([P, PIECE], F32, name="v_late", tag="squared")
-        look_up(2, N - PIECE, PIECE, v_late[:], squares[:, 2, late])
-        add_squares(PIECES - 1, squares[:, 2, late], stop=True)
         take_inverse(3)
 
         out_dqj = out.rearrange("(q d) j -> d q j", q=Q)

@@ -26,17 +26,17 @@ def tile_quaterniontransformer_kernel(tc, x, sc, ang, offs, out):
         tc.tile_pool(name="turn", bufs=3) as turn,
         tc.psum_pool(name="psum", bufs=1) as psum,
     ):
+        tables = [held.tile([P, VOCAB], F32, name=f"table{q}") for q in range(Q)]
+        nc.scalar.dma_start(tables[0][:], x[:P, :])
+
+        sc_rows = held.tile([Q, P], F32, name="sc_rows")
+        nc.sync.dma_start(sc_rows[:], sc.rearrange("(q d) o -> q (d o)", q=Q))
+
         offsets = held.tile([P, N // 16], U16, name="offsets")
         nc.sync.dma_start(offsets[:], offs)
 
-        sc_rows = held.tile([Q, P], F32, name="sc_rows")
-        nc.scalar.dma_start(sc_rows[:], sc.rearrange("(q d) o -> q (d o)", q=Q))
-
-        tables = []
-        for q in range(Q):
-            table = held.tile([P, VOCAB], F32, name=f"table{q}")
-            nc.sync.dma_start(table[:], x[q * P : (q + 1) * P, :])
-            tables.append(table)
+        for q in range(1, Q):
+            nc.sync.dma_start(tables[q][:], x[q * P : (q + 1) * P, :])
 
         angle = held.tile([P, N], F32, name="angle")
         nc.sync.dma_start(angle[:], ang)

import concourse.mybir as mybir
from concourse.masks import make_identity

P = 128
Q = 4
VOCAB = 2048
N = 1024
EPS = 1e-6
HALF = 512
PIECE = 256
PIECES = N // PIECE
WARMING = 8

F32 = mybir.dt.float32
U16 = mybir.dt.uint16
MULT = mybir.AluOpType.mult
FUNC = mybir.ActivationFunctionType


def tile_quaterniontransformer_kernel(tc, x, sc, ang, offs, out):
    nc = tc.nc
    with (
        tc.tile_pool(name="held", bufs=1) as held,
        tc.tile_pool(name="ring", bufs=PIECES) as ring,
        tc.tile_pool(name="slot", bufs=1) as slot,
        tc.tile_pool(name="turn", bufs=3) as turn,
        tc.psum_pool(name="psum", bufs=1) as psum,
    ):
        tables = [held.tile([P, VOCAB], F32, name=f"table{q}") for q in range(Q)]
        nc.scalar.dma_start(tables[0][:], x[:P, :])

        sc_rows = held.tile([Q, P], F32, name="sc_rows")
        nc.sync.dma_start(sc_rows[:], sc.rearrange("(q d) o -> q (d o)", q=Q))

        offsets = held.tile([P, N // 16], U16, name="offsets")
        nc.sync.dma_start(offsets[:], offs)

        for q in range(1, Q):
            nc.sync.dma_start(tables[q][:], x[q * P : (q + 1) * P, :])

        angle = held.tile([P, N], F32, name="angle")
        nc.sync.dma_start(angle[:], ang)

        ones = held.tile([P, 1], F32, name="ones")
        nc.gpsimd.memset(ones[:], 1.0)
        nc.scalar.activation(ones[:], ones[:], FUNC.Abs_reciprocal_sqrt)

        identity = held.tile([P, P], F32, name="identity")
        make_identity(nc, identity[:])

        sc_columns = psum.tile([P, Q], F32, name="sc_columns")
        nc.tensor.matmul(sc_columns[:], sc_rows[:], identity[:Q, :Q], start=True, stop=True)

        unread = psum.tile([P, P], F32, name="unread")
        for i in range(WARMING):
            nc.tensor.matmul(unread[:], identity[:], identity[:], start=True, stop=True)

        sc_spread = held.tile([P, Q, HALF], F32, name="sc_spread")
        for q in range(Q):
            nc.scalar.copy(sc_spread[:, q, :], sc_columns[:, q : q + 1].to_broadcast([P, HALF]))

        v = held.tile([P, Q, N], F32, name="v")
        squares = held.tile([P, Q - 1, N], F32, name="squares")
        norm2 = [psum.tile([P, PIECE], F32, name=f"norm2_{p}") for p in range(PIECES)]
        inverse = held.tile([P, N], F32, name="inverse")

        def look_up(q, first, width, looked_up, squared):
            nc.vector.tensor_tensor(
                looked_up,
                tables[q][:].indirect(offsets[:, first // 16 : (first + width) // 16]),
                sc_spread[:, q, :width],
                MULT,
            )
            nc.scalar.activation(squared, looked_up, FUNC.Square)

        def add_squares(p, squared, start=False, stop=False):
            nc.tensor.matmul(norm2[p][:], identity[:], squared, start=start, stop=stop)

        def take_inverse(p):
            nc.scalar.activation(
                inverse[:, p * PIECE : (p + 1) * PIECE], norm2[p][:], FUNC.Abs_reciprocal_sqrt, bias=EPS
            )

        def piece(p):
            return slice(p * PIECE, (p + 1) * PIECE)

        def look_up_in_turn(q, p, looked_up, stop):
            squared = turn.tile([P, PIECE], F32, name="squared")
            look_up(q, p * PIECE, PIECE, looked_up, squared[:])
            add_squares(p, squared[:], stop=stop)

        for q in (0, 1):
            for first in (0, HALF):
                half = slice(first, first + HALF)
                look_up(q, first, HALF, v[:, q, half], squares[:, q, half])
                for p in range(first // PIECE, (first + HALF) // PIECE):
                    add_squares(p, squares[:, q, piece(p)], start=(q == 0))
        look_up(2, 0, PIECE, v[:, 2, piece(0)], squares[:, 2, piece(0)])
        add_squares(0, squares[:, 2, piece(0)])
        squared1 = slot.tile([P, PIECE], F32, name="squared1", tag="slot")
        look_up(2, PIECE, PIECE, v[:, 2, piece(1)], squared1[:])
        add_squares(1, squared1[:])
        look_up(2, 2 * PIECE, PIECE, v[:, 2, piece(2)], squares[:, 2, piece(2)])

        look_up_in_turn(3, 0, v[:, 3, piece(0)], True)
        look_up_in_turn(3, 1, v[:, 3, piece(1)], True)
        add_squares(2, squares[:, 2, piece(2)])
        look_up_in_turn(3, 2, v[:, 3, piece(2)], True)
        take_inverse(0)
        look_up_in_turn(3, 3, v[:, 3, piece(3)], False)
        take_inverse(1)
        v_late = slot.tile([P, PIECE], F32, name="v_late", tag="slot")
        look_up_in_turn(2, 3, v_late[:], True)
        take_inverse(2)
        take_inverse(3)

        out_dqj = out.rearrange("(q d) j -> d q j", q=Q)
        for p in range(PIECES):
            first = p * PIECE
            cols = slice(first, first + PIECE)
            parts = [slice(0, PIECE // 4), slice(PIECE // 4, PIECE)]
            factor = ring.tile([P, PIECE], F32, name="factor")
            for part in parts:
                there = slice(first + part.start, first + part.stop)
                nc.vector.tensor_tensor(factor[:, part], inverse[:, there], angle[:, there], MULT)
            together = 1 if p == PIECES - 1 else 2 if p == PIECES - 2 else Q
            result = ring.tile([P, Q, PIECE], F32, name="result")
            for q in range(0, Q, together):
                group = slice(q, q + together)
                for part in parts if q == 0 else [slice(0, PIECE)]:
                    there = slice(first + part.start, first + part.stop)
                    held_back = q == 2 and p == PIECES - 1
                    looked_up = v_late[:, part].unsqueeze(1) if held_back else v[:, group, there]
                    spread = factor[:, part].unsqueeze(1).to_broadcast([P, together, part.stop - part.start])
                    nc.vector.tensor_tensor(result[:, group, part], looked_up, spread, MULT)
                nc.sync.dma_start(out_dqj[:, group, cols], result[:, group, :])
